import numpy as np
import ml_dtypes


def mxq(x, axis, fmt="e4m3"):
    dtype, down = {"e4m3": (ml_dtypes.float8_e4m3fn, 7), "e5m2": (ml_dtypes.float8_e5m2, 14)}[fmt]
    v = np.moveaxis(np.asarray(x, np.float32).astype(ml_dtypes.bfloat16).astype(np.float64), axis, -1)
    blocks = v.reshape(v.shape[:-1] + (-1, 32))
    amax = np.abs(blocks).max(-1, keepdims=True)
    byte = np.maximum(np.where(amax > 0, np.frexp(amax)[1] - 1 + 127, 0) - down, 1)
    scale = np.exp2(byte - 127.0)
    codes = (blocks / scale).astype(np.float32).astype(dtype).astype(np.float64)
    return np.moveaxis((codes * scale).reshape(v.shape), -1, axis)


WIDE = False


def mx_kscale(k):
    if not WIDE:
        return np.ones(k)
    levels = np.array([20, -20, 10, -10, 0])
    a = np.random.permutation(np.resize(levels, k // 512 * 4)).reshape(k // 512, 4)
    idx = np.arange(k)
    return np.exp2(a[idx // 512, idx % 128 // 32])


BF16 = ml_dtypes.bfloat16


def bf(x):
    return np.asarray(x, np.float32).astype(BF16)


def f64(x):
    return np.asarray(x).astype(np.float64)


B, HH, WW, C, NH, KD, WS, SS = 1, 32, 32, 512, 8, 64, 8, 4
GH, GW, T, F = HH // WS, WW // WS, WS * WS, NH * KD
N = B * GH * GW


def merge_windows(p):
    last = p.shape[-1]
    m = p.reshape(B, GH, GW, WS, WS, last).swapaxes(2, 3).reshape(B, HH, WW, last)
    return np.roll(m, shift=(SS, SS), axis=(1, 2))


def split_windows(g):
    last = g.shape[-1]
    m = np.roll(g, shift=(-SS, -SS), axis=(1, 2))
    return m.reshape(B, GH, WS, GW, WS, last).swapaxes(2, 3).reshape(N * T, last)


def setup_inputs():
    s = mx_kscale(N * T)
    s_win = s.reshape(N, T, 1, 1)
    s_img = merge_windows(s.reshape(N * T, 1))
    attn_ctx = np.random.standard_normal((N, T, NH, KD)) * 0.4 * s_win
    x = np.random.standard_normal((B, HH, WW, C))
    wo = np.random.standard_normal((NH, KD, C)) * 2.0 / np.sqrt(F)
    bo = np.random.standard_normal(C) * 0.3
    g = np.random.standard_normal((B, HH, WW, C)) * np.exp2(np.random.randint(-12, 1, (B, HH, WW, 1))) / s_img
    return {"attn_ctx": bf(attn_ctx), "x": bf(x), "wo": bf(wo), "bo": bf(bo), "grad_out": bf(g)}


def reference(attn_ctx, x, wo, bo, grad_out):
    o = f64(attn_ctx).reshape(N * T, F)
    gw = split_windows(f64(grad_out))
    d = mxq(o, 0, "e4m3").T @ mxq(gw, 0, "e5m2")
    return d.reshape(NH, KD, C)

@@ -1,0 +1,123 @@
+from concourse import mybir
+
+FLOPS = 2 * 1024 * 512 * 512
+BYTES = (1024 * 512 * 2) * 2 + 512 * 512 * 4
+
+BF16 = mybir.dt.bfloat16
+F32 = mybir.dt.float32
+U32 = mybir.dt.uint32
+U8 = mybir.dt.uint8
+E4M3X4 = mybir.dt.float8_e4m3fn_x4
+E5M2X4 = mybir.dt.float8_e5m2_x4
+
+P = 128
+PACK = 4
+PASSES = 2
+FEATURES = 512
+CHANNELS = 512
+M_TILE = 128
+RUN = PACK * CHANNELS
+IMAGE = 32
+WINDOW = 8
+SHIFT = 4
+SPLIT = 256
+
+
+def load_half_window(nc, g_raw, grad_out, gi, gj, half):
+    first_partition = 64 * (gi % 2) + 16 * gj + half
+    first_row = (WINDOW * gi + SHIFT) % IMAGE
+    column = (WINDOW * gj + PACK * half + SHIFT) % IMAGE
+    rows_before_wrap = min(WINDOW, IMAGE - first_row)
+    for ti, row, count in (
+        (0, first_row, rows_before_wrap),
+        (rows_before_wrap, 0, WINDOW - rows_before_wrap),
+    ):
+        if count > 0:
+            nc.sync.dma_start(
+                out=g_raw[first_partition + 2 * ti : first_partition + 2 * (ti + count) - 1 : 2, :],
+                in_=grad_out[0, row : row + count, column : column + PACK, :].rearrange(
+                    "i v c -> i (v c)"
+                ),
+            )
+
+
+def regroup(nc, grouped, raw):
+    for engine_copy, cols in (
+        (nc.vector.tensor_copy, slice(0, SPLIT)),
+        (nc.scalar.copy, slice(SPLIT, CHANNELS)),
+    ):
+        engine_copy(
+            out=grouped[:, cols, :].rearrange("p (c i) j -> p c j i", i=4),
+            in_=raw[:, :, cols].rearrange("p j (c i) -> p c j i", i=4),
+        )
+
+
+def tile_windowattentionblock_pb_s_kernel(tc, attn_ctx, x, wo, bo, grad_out, out):
+    nc = tc.nc
+    attn_runs = attn_ctx.rearrange("n t h d -> (n t) (h d)").rearrange(
+        "(s p j) f -> s p (j f)", s=PASSES, p=P, j=PACK
+    )
+    out_rows = out.rearrange("h d c -> (h d) c")
+
+    with tc.tile_pool(name="keep", bufs=1) as keep, tc.psum_pool(name="psum", bufs=1) as psum:
+        attn_raw = []
+        grad_raw = []
+        for s in range(PASSES):
+            a_raw = keep.tile([P, RUN], BF16, name="a_raw%d" % s)
+            nc.sync.dma_start(out=a_raw[:], in_=attn_runs[s])
+            attn_raw.append(a_raw)
+            g_raw = keep.tile([P, RUN], BF16, name="g_raw%d" % s)
+            for gi in (2 * s, 2 * s + 1):
+                for gj in range(IMAGE // WINDOW):
+                    for half in range(2):
+                        load_half_window(nc, g_raw, grad_out, gi, gj, half)
+            grad_raw.append(g_raw)
+
+        attn_codes, attn_scales, grad_codes, grad_scales = [], [], [], []
+        for s in range(PASSES):
+            a_grouped = keep.tile([P, FEATURES, PACK], BF16, name="a_grouped%d" % s, align_bytes=64)
+            regroup(nc, a_grouped, attn_raw[s][:].rearrange("p (j w) -> p j w", j=PACK))
+            g_grouped = keep.tile([P, CHANNELS, PACK], BF16, name="g_grouped%d" % s, align_bytes=64)
+            regroup(nc, g_grouped, grad_raw[s][:].rearrange("p (j w) -> p j w", j=PACK))
+
+            a_codes = keep.tile([P, FEATURES], U32, name="a_codes%d" % s, align_bytes=64)
+            a_scales = keep.tile([P, FEATURES], U8, name="a_scales%d" % s, align_bytes=64)
+            nc.vector.quantize_mx(
+                out=a_codes[:].bitcast(E4M3X4),
+                scales=a_scales[:],
+                in_=a_grouped[:].rearrange("p w j -> p (w j)"),
+            )
+            g_codes = keep.tile([P, CHANNELS], U32, name="g_codes%d" % s, align_bytes=64)
+            g_scales = keep.tile([P, CHANNELS], U8, name="g_scales%d" % s, align_bytes=64)
+            nc.vector.quantize_mx(
+                out=g_codes[:].bitcast(E5M2X4),
+                scales=g_scales[:],
+                in_=g_grouped[:].rearrange("p w j -> p (w j)"),
+            )
+            attn_codes.append(a_codes)
+            attn_scales.append(a_scales)
+            grad_codes.append(g_codes)
+            grad_scales.append(g_scales)
+
+        m_tiles = FEATURES // M_TILE
+        acc = [psum.tile([M_TILE, CHANNELS], F32, name="acc%d" % m) for m in range(m_tiles)]
+        for s in range(PASSES):
+            for m in range(m_tiles):
+                m_cols = slice(m * M_TILE, (m + 1) * M_TILE)
+                nc.tensor.matmul_mx(
+                    out=acc[m][:],
+                    lhsT=attn_codes[s][:, m_cols].bitcast(E4M3X4),
+                    lhsT_scale=attn_scales[s][:, m_cols],
+                    rhs=grad_codes[s][:].bitcast(E5M2X4),
+                    rhs_scale=grad_scales[s][:],
+                    start=(s == 0),
+                    stop=(s == PASSES - 1),
+                )
+
+        for m in range(m_tiles):
+            result = keep.tile([M_TILE, CHANNELS], F32, name="result%d" % m)
+            if m % 2 == 0:
+                nc.scalar.copy(out=result[:], in_=acc[m][:])
+            else:
+                nc.vector.tensor_copy(out=result[:], in_=acc[m][:])
+            nc.sync.dma_start(out=out_rows[m * M_TILE : (m + 1) * M_TILE, :], in_=result[:])

@@ -24,6 +24,7 @@ SPLIT = 256
 
 
 def load_half_window(nc, g_raw, grad_out, gi, gj, half):
+    queue = nc.sync if gi % 2 == 0 else nc.scalar
     first_partition = 64 * (gi % 2) + 16 * gj + half
     first_row = (WINDOW * gi + SHIFT) % IMAGE
     column = (WINDOW * gj + PACK * half + SHIFT) % IMAGE
@@ -33,7 +34,7 @@ def load_half_window(nc, g_raw, grad_out, gi, gj, half):
         (rows_before_wrap, 0, WINDOW - rows_before_wrap),
     ):
         if count > 0:
-            nc.sync.dma_start(
+            queue.dma_start(
                 out=g_raw[first_partition + 2 * ti : first_partition + 2 * (ti + count) - 1 : 2, :],
                 in_=grad_out[0, row : row + count, column : column + PACK, :].rearrange(
                     "i v c -> i (v c)"
@@ -64,12 +65,12 @@ def tile_windowattentionblock_pb_s_kernel(tc, attn_ctx, x, wo, bo, grad_out, out
         grad_raw = []
         for s in range(PASSES):
             a_raw = keep.tile([P, RUN], BF16, name="a_raw%d" % s)
-            nc.sync.dma_start(out=a_raw[:], in_=attn_runs[s])
+            nc.gpsimd.dma_start(out=a_raw[:], in_=attn_runs[s])
             attn_raw.append(a_raw)
             g_raw = keep.tile([P, RUN], BF16, name="g_raw%d" % s)
-            for gi in (2 * s, 2 * s + 1):
+            for half in range(2):
                 for gj in range(IMAGE // WINDOW):
-                    for half in range(2):
+                    for gi in (2 * s, 2 * s + 1):
                         load_half_window(nc, g_raw, grad_out, gi, gj, half)
             grad_raw.append(g_raw)
 

@@ -1,4 +1,5 @@
 from concourse import mybir
+from concourse.masks import make_identity
 
 FLOPS = 2 * 1024 * 512 * 512
 BYTES = (1024 * 512 * 2) * 2 + 512 * 512 * 4
@@ -18,39 +19,41 @@ CHANNELS = 512
 M_TILE = 128
 RUN = PACK * CHANNELS
 IMAGE = 32
-WINDOW = 8
 SHIFT = 4
-SPLIT = 256
+PASS_ROWS = IMAGE // PASSES
+RUNS_PER_ROW = IMAGE // PACK
+HALVES = 2
+HALF = CHANNELS // HALVES
+ATTN_SPLIT = 192
 
 
-def load_half_window(nc, g_raw, grad_out, gi, gj, half):
-    queue = nc.sync if gi % 2 == 0 else nc.scalar
-    first_partition = 64 * (gi % 2) + 16 * gj + half
-    first_row = (WINDOW * gi + SHIFT) % IMAGE
-    column = (WINDOW * gj + PACK * half + SHIFT) % IMAGE
-    rows_before_wrap = min(WINDOW, IMAGE - first_row)
-    for ti, row, count in (
-        (0, first_row, rows_before_wrap),
-        (rows_before_wrap, 0, WINDOW - rows_before_wrap),
-    ):
-        if count > 0:
-            queue.dma_start(
-                out=g_raw[first_partition + 2 * ti : first_partition + 2 * (ti + count) - 1 : 2, :],
-                in_=grad_out[0, row : row + count, column : column + PACK, :].rearrange(
-                    "i v c -> i (v c)"
-                ),
-            )
+def window_order_permutation(nc, pool, ident):
+    perm = pool.tile([P, P], F32, name="perm")
+    to_window = perm[:].rearrange("q (a g t h) -> q h a g t", a=2, g=4, t=8, h=2)
+    from_image = ident[:].rearrange("q (a t g e) -> q e a g t", a=2, t=8, g=4, e=2)
+    nc.vector.tensor_copy(out=to_window[:, 0], in_=from_image[:, 1])
+    nc.vector.tensor_copy(out=to_window[:, 1, :, 0:3, :], in_=from_image[:, 0, :, 1:4, :])
+    nc.vector.tensor_copy(out=to_window[:, 1, :, 3:4, :], in_=from_image[:, 0, :, 0:1, :])
+    return perm
 
 
-def regroup(nc, grouped, raw):
-    for engine_copy, cols in (
-        (nc.vector.tensor_copy, slice(0, SPLIT)),
-        (nc.scalar.copy, slice(SPLIT, CHANNELS)),
-    ):
-        engine_copy(
-            out=grouped[:, cols, :].rearrange("p (c i) j -> p c j i", i=4),
-            in_=raw[:, :, cols].rearrange("p j (c i) -> p c j i", i=4),
-        )
+def copy_out(nc, half, out, in_):
+    if half == 0:
+        nc.vector.tensor_copy(out=out, in_=in_)
+    else:
+        nc.scalar.copy(out=out, in_=in_)
+
+
+def quantise(nc, pool, name, grouped, x4_dtype):
+    columns = grouped.shape[1]
+    codes = pool.tile([P, columns], U32, name=name + "_codes", align_bytes=64)
+    scales = pool.tile([P, columns], U8, name=name + "_scales", align_bytes=64)
+    nc.vector.quantize_mx(
+        out=codes[:].bitcast(x4_dtype),
+        scales=scales[:],
+        in_=grouped[:].rearrange("p w j -> p (w j)"),
+    )
+    return codes, scales
 
 
 def tile_windowattentionblock_pb_s_kernel(tc, attn_ctx, x, wo, bo, grad_out, out):
@@ -58,62 +61,103 @@ def tile_windowattentionblock_pb_s_kernel(tc, attn_ctx, x, wo, bo, grad_out, out
     attn_runs = attn_ctx.rearrange("n t h d -> (n t) (h d)").rearrange(
         "(s p j) f -> s p (j f)", s=PASSES, p=P, j=PACK
     )
+    grad_runs = grad_out.rearrange("b i (q v) c -> (b i q) (v c)", v=PACK)
     out_rows = out.rearrange("h d c -> (h d) c")
+    m_tiles = FEATURES // M_TILE
 
-    with tc.tile_pool(name="keep", bufs=1) as keep, tc.psum_pool(name="psum", bufs=1) as psum:
-        attn_raw = []
+    with tc.tile_pool(name="keep", bufs=1) as keep, tc.psum_pool(
+        name="sums", bufs=1
+    ) as sums, tc.psum_pool(name="turns", bufs=4) as turns, tc.manual_schedule():
+
         grad_raw = []
         for s in range(PASSES):
-            a_raw = keep.tile([P, RUN], BF16, name="a_raw%d" % s)
-            nc.gpsimd.dma_start(out=a_raw[:], in_=attn_runs[s])
-            attn_raw.append(a_raw)
             g_raw = keep.tile([P, RUN], BF16, name="g_raw%d" % s)
-            for half in range(2):
-                for gj in range(IMAGE // WINDOW):
-                    for gi in (2 * s, 2 * s + 1):
-                        load_half_window(nc, g_raw, grad_out, gi, gj, half)
+            first_row = SHIFT + PASS_ROWS * s
+            rows = min(PASS_ROWS, IMAGE - first_row)
+            nc.sync.dma_start(
+                out=g_raw[0 : rows * RUNS_PER_ROW, :],
+                in_=grad_runs[first_row * RUNS_PER_ROW : (first_row + rows) * RUNS_PER_ROW, :],
+            )
+            if rows < PASS_ROWS:
+                nc.sync.dma_start(
+                    out=g_raw[rows * RUNS_PER_ROW : P, :],
+                    in_=grad_runs[0 : (PASS_ROWS - rows) * RUNS_PER_ROW, :],
+                )
             grad_raw.append(g_raw)
-
-        attn_codes, attn_scales, grad_codes, grad_scales = [], [], [], []
+        attn_raw = []
         for s in range(PASSES):
-            a_grouped = keep.tile([P, FEATURES, PACK], BF16, name="a_grouped%d" % s, align_bytes=64)
-            regroup(nc, a_grouped, attn_raw[s][:].rearrange("p (j w) -> p j w", j=PACK))
+            a_raw = keep.tile([P, RUN], BF16, name="a_raw%d" % s)
+            nc.sync.dma_start(out=a_raw[:], in_=attn_runs[s])
+            attn_raw.append(a_raw)
+
+        ident = keep.tile([P, P], F32, name="ident")
+        make_identity(nc, ident[:])
+        perm = window_order_permutation(nc, keep, ident)
+
+        def first_turn(s):
+            words = grad_raw[s][:].bitcast(F32).rearrange("q (j e w) -> q j e w", j=PACK, e=HALVES)
+            turned = []
+            for half in range(HALVES):
+                bank = turns.tile([P, PACK, P], F32, name="bank")
+                for j in range(PACK):
+                    nc.tensor.transpose(out=bank[:, j, :], in_=words[:, j, half, :], identity=perm[:])
+                turned.append(keep.tile([P, PACK, P], F32, name="turned%d%d" % (s, half)))
+                copy_out(nc, half, turned[half][:], bank[:])
+            return turned
+
+        def second_turn(s, turned):
             g_grouped = keep.tile([P, CHANNELS, PACK], BF16, name="g_grouped%d" % s, align_bytes=64)
-            regroup(nc, g_grouped, grad_raw[s][:].rearrange("p (j w) -> p j w", j=PACK))
+            for half in range(HALVES):
+                bank = turns.tile([P, PACK, P], F32, name="bank")
+                for j in range(PACK):
+                    nc.tensor.transpose(out=bank[:, j, :], in_=turned[half][:, j, :], identity=ident[:])
+                copy_out(
+                    nc,
+                    half,
+                    g_grouped[:, half * HALF : (half + 1) * HALF, :],
+                    bank[:].bitcast(BF16).rearrange("p j c -> p c j"),
+                )
+            return g_grouped
 
-            a_codes = keep.tile([P, FEATURES], U32, name="a_codes%d" % s, align_bytes=64)
-            a_scales = keep.tile([P, FEATURES], U8, name="a_scales%d" % s, align_bytes=64)
-            nc.vector.quantize_mx(
-                out=a_codes[:].bitcast(E4M3X4),
-                scales=a_scales[:],
-                in_=a_grouped[:].rearrange("p w j -> p (w j)"),
-            )
-            g_codes = keep.tile([P, CHANNELS], U32, name="g_codes%d" % s, align_bytes=64)
-            g_scales = keep.tile([P, CHANNELS], U8, name="g_scales%d" % s, align_bytes=64)
-            nc.vector.quantize_mx(
-                out=g_codes[:].bitcast(E5M2X4),
-                scales=g_scales[:],
-                in_=g_grouped[:].rearrange("p w j -> p (w j)"),
-            )
-            attn_codes.append(a_codes)
-            attn_scales.append(a_scales)
-            grad_codes.append(g_codes)
-            grad_scales.append(g_scales)
+        def regroup_attn(s):
+            a_grouped = keep.tile([P, FEATURES, PACK], BF16, name="a_grouped%d" % s, align_bytes=64)
+            a_tokens = attn_raw[s][:].rearrange("p (j w) -> p j w", j=PACK)
+            for engine_copy, cols in (
+                (nc.vector.tensor_copy, slice(0, ATTN_SPLIT)),
+                (nc.scalar.copy, slice(ATTN_SPLIT, FEATURES)),
+            ):
+                engine_copy(
+                    out=a_grouped[:, cols, :].rearrange("p (c i) j -> p c j i", i=4),
+                    in_=a_tokens[:, :, cols].rearrange("p j (c i) -> p c j i", i=4),
+                )
+            return a_grouped
 
-        m_tiles = FEATURES // M_TILE
-        acc = [psum.tile([M_TILE, CHANNELS], F32, name="acc%d" % m) for m in range(m_tiles)]
-        for s in range(PASSES):
+        acc = [sums.tile([M_TILE, CHANNELS], F32, name="acc%d" % m) for m in range(m_tiles)]
+
+        def multiply(s, attn_mx, grad_mx):
             for m in range(m_tiles):
                 m_cols = slice(m * M_TILE, (m + 1) * M_TILE)
                 nc.tensor.matmul_mx(
                     out=acc[m][:],
-                    lhsT=attn_codes[s][:, m_cols].bitcast(E4M3X4),
-                    lhsT_scale=attn_scales[s][:, m_cols],
-                    rhs=grad_codes[s][:].bitcast(E5M2X4),
-                    rhs_scale=grad_scales[s][:],
+                    lhsT=attn_mx[0][:, m_cols].bitcast(E4M3X4),
+                    lhsT_scale=attn_mx[1][:, m_cols],
+                    rhs=grad_mx[0][:].bitcast(E5M2X4),
+                    rhs_scale=grad_mx[1][:],
                     start=(s == 0),
                     stop=(s == PASSES - 1),
                 )
+
+        g_grouped0 = second_turn(0, first_turn(0))
+        turned1 = first_turn(1)
+        grad_mx0 = quantise(nc, keep, "g0", g_grouped0, E5M2X4)
+        g_grouped1 = second_turn(1, turned1)
+        a_grouped0 = regroup_attn(0)
+        a_grouped1 = regroup_attn(1)
+        grad_mx1 = quantise(nc, keep, "g1", g_grouped1, E5M2X4)
+        attn_mx0 = quantise(nc, keep, "a0", a_grouped0, E4M3X4)
+        multiply(0, attn_mx0, grad_mx0)
+        attn_mx1 = quantise(nc, keep, "a1", a_grouped1, E4M3X4)
+        multiply(1, attn_mx1, grad_mx1)
 
         for m in range(m_tiles):
             result = keep.tile([M_TILE, CHANNELS], F32, name="result%d" % m)

@@ -18,42 +18,19 @@ FEATURES = 512
 CHANNELS = 512
 M_TILE = 128
 RUN = PACK * CHANNELS
-IMAGE = 32
-SHIFT = 4
-PASS_ROWS = IMAGE // PASSES
-RUNS_PER_ROW = IMAGE // PACK
-HALVES = 2
-HALF = CHANNELS // HALVES
-ATTN_SPLIT = 192
+GROUPS = 4
+CHUNKS = CHANNELS // P
 
 
 def window_order_permutation(nc, pool, ident):
-    perm = pool.tile([P, P], F32, name="perm")
-    to_window = perm[:].rearrange("q (a g t h) -> q h a g t", a=2, g=4, t=8, h=2)
-    from_image = ident[:].rearrange("q (a t g e) -> q e a g t", a=2, t=8, g=4, e=2)
-    nc.vector.tensor_copy(out=to_window[:, 0], in_=from_image[:, 1])
-    nc.vector.tensor_copy(out=to_window[:, 1, :, 0:3, :], in_=from_image[:, 0, :, 1:4, :])
-    nc.vector.tensor_copy(out=to_window[:, 1, :, 3:4, :], in_=from_image[:, 0, :, 0:1, :])
+    perm = pool.tile([P, P], BF16, name="perm")
+    to_token = perm[:].rearrange("q (u g r h v) -> q u h g r v", u=2, g=4, r=4, h=2, v=2)
+    from_pixel = ident[:].rearrange("q (r g e u v) -> q u e g r v", r=4, g=4, e=2, u=2, v=2)
+    for u in range(2):
+        nc.vector.tensor_copy(out=to_token[:, u, 0], in_=from_pixel[:, u, 1])
+        nc.vector.tensor_copy(out=to_token[:, u, 1, 0:3], in_=from_pixel[:, u, 0, 1:4])
+        nc.vector.tensor_copy(out=to_token[:, u, 1, 3:4], in_=from_pixel[:, u, 0, 0:1])
     return perm
-
-
-def copy_out(nc, half, out, in_):
-    if half == 0:
-        nc.vector.tensor_copy(out=out, in_=in_)
-    else:
-        nc.scalar.copy(out=out, in_=in_)
-
-
-def quantise(nc, pool, name, grouped, x4_dtype):
-    columns = grouped.shape[1]
-    codes = pool.tile([P, columns], U32, name=name + "_codes", align_bytes=64)
-    scales = pool.tile([P, columns], U8, name=name + "_scales", align_bytes=64)
-    nc.vector.quantize_mx(
-        out=codes[:].bitcast(x4_dtype),
-        scales=scales[:],
-        in_=grouped[:].rearrange("p w j -> p (w j)"),
-    )
-    return codes, scales
 
 
 def tile_windowattentionblock_pb_s_kernel(tc, attn_ctx, x, wo, bo, grad_out, out):
@@ -61,7 +38,7 @@ def tile_windowattentionblock_pb_s_kernel(tc, attn_ctx, x, wo, bo, grad_out, out
     attn_runs = attn_ctx.rearrange("n t h d -> (n t) (h d)").rearrange(
         "(s p j) f -> s p (j f)", s=PASSES, p=P, j=PACK
     )
-    grad_runs = grad_out.rearrange("b i (q v) c -> (b i q) (v c)", v=PACK)
+    grad_px = grad_out.rearrange("b (t r) j c -> (b r j) t c", r=4)
     out_rows = out.rearrange("h d c -> (h d) c")
     m_tiles = FEATURES // M_TILE
 
@@ -69,100 +46,179 @@ def tile_windowattentionblock_pb_s_kernel(tc, attn_ctx, x, wo, bo, grad_out, out
         name="sums", bufs=1
     ) as sums, tc.psum_pool(name="turns", bufs=4) as turns, tc.manual_schedule():
 
-        grad_raw = []
-        for s in range(PASSES):
-            g_raw = keep.tile([P, RUN], BF16, name="g_raw%d" % s)
-            first_row = SHIFT + PASS_ROWS * s
-            rows = min(PASS_ROWS, IMAGE - first_row)
-            nc.sync.dma_start(
-                out=g_raw[0 : rows * RUNS_PER_ROW, :],
-                in_=grad_runs[first_row * RUNS_PER_ROW : (first_row + rows) * RUNS_PER_ROW, :],
-            )
-            if rows < PASS_ROWS:
-                nc.sync.dma_start(
-                    out=g_raw[rows * RUNS_PER_ROW : P, :],
-                    in_=grad_runs[0 : (PASS_ROWS - rows) * RUNS_PER_ROW, :],
-                )
-            grad_raw.append(g_raw)
-        attn_raw = []
-        for s in range(PASSES):
+        def copy_on(engine, out_ap, in_ap):
+            if engine == "V":
+                nc.vector.tensor_copy(out=out_ap, in_=in_ap)
+            else:
+                nc.scalar.copy(out=out_ap, in_=in_ap)
+
+        def load_grad(name, first_group, groups):
+            raw = keep.tile([P, groups, CHANNELS], BF16, name=name)
+            nc.sync.dma_start(out=raw[:], in_=grad_px[:, first_group : first_group + groups, :])
+            return raw
+
+        def load_attn(s):
             a_raw = keep.tile([P, RUN], BF16, name="a_raw%d" % s)
             nc.sync.dma_start(out=a_raw[:], in_=attn_runs[s])
-            attn_raw.append(a_raw)
+            return a_raw
 
-        ident = keep.tile([P, P], F32, name="ident")
-        make_identity(nc, ident[:])
-        perm = window_order_permutation(nc, keep, ident)
+        g0a = load_grad("g0a", 1, 2)
+        g0b = load_grad("g0b", 3, 2)
+        a_raw0 = load_attn(0)
+        g1a = load_grad("g1a", 5, 3)
+        g1b = load_grad("g1b", 0, 1)
+        a_raw1 = load_attn(1)
+        attn_raw = [a_raw0, a_raw1]
+        grad_group = [
+            [(g0a, 0), (g0a, 1), (g0b, 0), (g0b, 1)],
+            [(g1a, 0), (g1a, 1), (g1a, 2), (g1b, 0)],
+        ]
 
-        def first_turn(s):
-            words = grad_raw[s][:].bitcast(F32).rearrange("q (j e w) -> q j e w", j=PACK, e=HALVES)
-            turned = []
-            for half in range(HALVES):
-                bank = turns.tile([P, PACK, P], F32, name="bank")
-                for j in range(PACK):
-                    nc.tensor.transpose(out=bank[:, j, :], in_=words[:, j, half, :], identity=perm[:])
-                turned.append(keep.tile([P, PACK, P], F32, name="turned%d%d" % (s, half)))
-                copy_out(nc, half, turned[half][:], bank[:])
-            return turned
+        ident16 = keep.tile([P, P], BF16, name="ident16")
+        make_identity(nc, ident16[:])
+        perm = window_order_permutation(nc, keep, ident16)
+        ident32 = keep.tile([P, P], F32, name="ident32")
+        make_identity(nc, ident32[:])
 
-        def second_turn(s, turned):
-            g_grouped = keep.tile([P, CHANNELS, PACK], BF16, name="g_grouped%d" % s, align_bytes=64)
-            for half in range(HALVES):
-                bank = turns.tile([P, PACK, P], F32, name="bank")
-                for j in range(PACK):
-                    nc.tensor.transpose(out=bank[:, j, :], in_=turned[half][:, j, :], identity=ident[:])
-                copy_out(
-                    nc,
-                    half,
-                    g_grouped[:, half * HALF : (half + 1) * HALF, :],
-                    bank[:].bitcast(BF16).rearrange("p j c -> p c j"),
-                )
-            return g_grouped
+        by_channel = [keep.tile([P, 2 * CHUNKS, P], F32, name="by_channel%d" % s) for s in range(PASSES)]
+        first_banks = {}
 
-        def regroup_attn(s):
-            a_grouped = keep.tile([P, FEATURES, PACK], BF16, name="a_grouped%d" % s, align_bytes=64)
+        def first_turn(s, t):
+            raw, i = grad_group[s][t]
+            bank = turns.tile([P, CHUNKS, P], BF16, name="bank")
+            for k in range(CHUNKS):
+                nc.tensor.transpose(out=bank[:, k, :], in_=raw[:, i, k * P : (k + 1) * P], identity=perm[:])
+            first_banks[(s, t)] = bank
+
+        def first_copy(s, t, engine):
+            bank = first_banks[(s, t)]
+            words = bank[:].rearrange("c k n -> c (k n)").bitcast(F32)
+            half, u = divmod(t, 2)
+            dest = by_channel[s][:, :, half * 64 : (half + 1) * 64].rearrange(
+                "c y (g u w) -> c y g u w", g=4, u=2, w=8
+            )
+            copy_on(engine, dest[:, :, :, u, :], words.rearrange("c (y g w) -> c y g w", g=4, w=8))
+
+        second_banks = {}
+
+        def second_turn(s, b):
+            bank = turns.tile([P, 2, 2, P], F32, name="bank")
+            for k in range(2):
+                for u in range(2):
+                    nc.tensor.transpose(
+                        out=bank[:, k, u, :], in_=by_channel[s][:, 2 * (2 * b + k) + u, :], identity=ident32[:]
+                    )
+            second_banks[(s, b)] = bank
+
+        g_grouped = [
+            [keep.tile([P, 2 * P, PACK], BF16, name="g_grouped%d%d" % (s, b), align_bytes=64) for b in range(2)]
+            for s in range(PASSES)
+        ]
+
+        def second_copy(s, b, engine):
+            bank = second_banks[(s, b)]
+            dest = g_grouped[s][b][:].rearrange("p c j -> p (c j)").bitcast(F32)
+            copy_on(
+                engine,
+                dest.rearrange("p (k c u) -> p k c u", k=2, u=2),
+                bank[:].rearrange("p k u c -> p k c u"),
+            )
+
+        g_codes = [keep.tile([P, CHANNELS], U32, name="g_codes%d" % s, align_bytes=64) for s in range(PASSES)]
+        g_scales = [keep.tile([P, CHANNELS], U8, name="g_scales%d" % s, align_bytes=64) for s in range(PASSES)]
+        a_codes = [keep.tile([P, FEATURES], U32, name="a_codes%d" % s, align_bytes=64) for s in range(PASSES)]
+        a_scales = [keep.tile([P, FEATURES], U8, name="a_scales%d" % s, align_bytes=64) for s in range(PASSES)]
+
+        def quantise_grad(s, b):
+            cols = slice(b * 2 * P, (b + 1) * 2 * P)
+            nc.vector.quantize_mx(
+                out=g_codes[s][:, cols].bitcast(E5M2X4),
+                scales=g_scales[s][:, cols],
+                in_=g_grouped[s][b][:].rearrange("p c j -> p (c j)"),
+            )
+
+        a_grouped = [
+            keep.tile([P, FEATURES, PACK], BF16, name="a_grouped%d" % s, align_bytes=64) for s in range(PASSES)
+        ]
+
+        def regroup_attn(s, m0, m1, engine):
+            cols = slice(m0 * M_TILE, m1 * M_TILE)
             a_tokens = attn_raw[s][:].rearrange("p (j w) -> p j w", j=PACK)
-            for engine_copy, cols in (
-                (nc.vector.tensor_copy, slice(0, ATTN_SPLIT)),
-                (nc.scalar.copy, slice(ATTN_SPLIT, FEATURES)),
-            ):
-                engine_copy(
-                    out=a_grouped[:, cols, :].rearrange("p (c i) j -> p c j i", i=4),
-                    in_=a_tokens[:, :, cols].rearrange("p j (c i) -> p c j i", i=4),
-                )
-            return a_grouped
+            copy_on(
+                engine,
+                a_grouped[s][:, cols, :].rearrange("p (c i) j -> p c j i", i=4),
+                a_tokens[:, :, cols].rearrange("p j (c i) -> p c j i", i=4),
+            )
+
+        def quantise_attn(s, m0, m1):
+            cols = slice(m0 * M_TILE, m1 * M_TILE)
+            nc.vector.quantize_mx(
+                out=a_codes[s][:, cols].bitcast(E4M3X4),
+                scales=a_scales[s][:, cols],
+                in_=a_grouped[s][:, cols, :].rearrange("p w j -> p (w j)"),
+            )
 
         acc = [sums.tile([M_TILE, CHANNELS], F32, name="acc%d" % m) for m in range(m_tiles)]
 
-        def multiply(s, attn_mx, grad_mx):
-            for m in range(m_tiles):
-                m_cols = slice(m * M_TILE, (m + 1) * M_TILE)
-                nc.tensor.matmul_mx(
-                    out=acc[m][:],
-                    lhsT=attn_mx[0][:, m_cols].bitcast(E4M3X4),
-                    lhsT_scale=attn_mx[1][:, m_cols],
-                    rhs=grad_mx[0][:].bitcast(E5M2X4),
-                    rhs_scale=grad_mx[1][:],
-                    start=(s == 0),
-                    stop=(s == PASSES - 1),
-                )
+        def multiply(s, m):
+            m_cols = slice(m * M_TILE, (m + 1) * M_TILE)
+            nc.tensor.matmul_mx(
+                out=acc[m][:],
+                lhsT=a_codes[s][:, m_cols].bitcast(E4M3X4),
+                lhsT_scale=a_scales[s][:, m_cols],
+                rhs=g_codes[s][:].bitcast(E5M2X4),
+                rhs_scale=g_scales[s][:],
+                start=(s == 0),
+                stop=(s == PASSES - 1),
+            )
 
-        g_grouped0 = second_turn(0, first_turn(0))
-        turned1 = first_turn(1)
-        grad_mx0 = quantise(nc, keep, "g0", g_grouped0, E5M2X4)
-        g_grouped1 = second_turn(1, turned1)
-        a_grouped0 = regroup_attn(0)
-        a_grouped1 = regroup_attn(1)
-        grad_mx1 = quantise(nc, keep, "g1", g_grouped1, E5M2X4)
-        attn_mx0 = quantise(nc, keep, "a0", a_grouped0, E4M3X4)
-        multiply(0, attn_mx0, grad_mx0)
-        attn_mx1 = quantise(nc, keep, "a1", a_grouped1, E4M3X4)
-        multiply(1, attn_mx1, grad_mx1)
-
-        for m in range(m_tiles):
+        def store(m, engine):
             result = keep.tile([M_TILE, CHANNELS], F32, name="result%d" % m)
-            if m % 2 == 0:
-                nc.scalar.copy(out=result[:], in_=acc[m][:])
-            else:
-                nc.vector.tensor_copy(out=result[:], in_=acc[m][:])
+            copy_on(engine, result[:], acc[m][:])
             nc.sync.dma_start(out=out_rows[m * M_TILE : (m + 1) * M_TILE, :], in_=result[:])
+
+        for t in range(GROUPS):
+            first_turn(0, t)
+        first_copy(0, 0, "S")
+        first_copy(0, 1, "V")
+        first_copy(0, 2, "S")
+        first_copy(0, 3, "V")
+        second_turn(0, 0)
+        second_turn(0, 1)
+        regroup_attn(0, 0, 2, "V")
+        for t in range(GROUPS):
+            first_turn(1, t)
+        second_copy(0, 0, "S")
+        second_copy(0, 1, "S")
+        regroup_attn(0, 2, 4, "V")
+        first_copy(1, 0, "S")
+        first_copy(1, 1, "S")
+        first_copy(1, 2, "S")
+        quantise_attn(0, 0, 4)
+        first_copy(1, 3, "V")
+        quantise_grad(0, 0)
+        quantise_grad(0, 1)
+        second_turn(1, 0)
+        second_turn(1, 1)
+        for m in range(m_tiles):
+            multiply(0, m)
+        regroup_attn(1, 0, 1, "V")
+        regroup_attn(1, 1, 2, "V")
+        quantise_attn(1, 0, 1)
+        quantise_attn(1, 1, 2)
+        second_copy(1, 0, "S")
+        second_copy(1, 1, "S")
+        quantise_grad(1, 0)
+        regroup_attn(1, 2, 3, "V")
+        quantise_grad(1, 1)
+        multiply(1, 0)
+        multiply(1, 1)
+        quantise_attn(1, 2, 3)
+        multiply(1, 2)
+        store(0, "S")
+        regroup_attn(1, 3, 4, "V")
+        store(1, "S")
+        quantise_attn(1, 3, 4)
+        multiply(1, 3)
+        store(2, "V")
+        store(3, "S")

@@ -42,9 +42,7 @@ def tile_windowattentionblock_pb_s_kernel(tc, attn_ctx, x, wo, bo, grad_out, out
     out_rows = out.rearrange("h d c -> (h d) c")
     m_tiles = FEATURES // M_TILE
 
-    with tc.tile_pool(name="keep", bufs=1) as keep, tc.psum_pool(
-        name="sums", bufs=1
-    ) as sums, tc.psum_pool(name="turns", bufs=4) as turns, tc.manual_schedule():
+    with tc.tile_pool(name="keep", bufs=1) as keep, tc.psum_pool(name="turns", bufs=8) as turns, tc.manual_schedule():
 
         def copy_on(engine, out_ap, in_ap):
             if engine == "V":
@@ -62,7 +60,8 @@ def tile_windowattentionblock_pb_s_kernel(tc, attn_ctx, x, wo, bo, grad_out, out
             nc.sync.dma_start(out=a_raw[:], in_=attn_runs[s])
             return a_raw
 
-        g0a = load_grad("g0a", 1, 2)
+        g00 = load_grad("g00", 1, 1)
+        g01 = load_grad("g01", 2, 1)
         g0b = load_grad("g0b", 3, 2)
         a_raw0 = load_attn(0)
         g1a = load_grad("g1a", 5, 3)
@@ -70,7 +69,7 @@ def tile_windowattentionblock_pb_s_kernel(tc, attn_ctx, x, wo, bo, grad_out, out
         a_raw1 = load_attn(1)
         attn_raw = [a_raw0, a_raw1]
         grad_group = [
-            [(g0a, 0), (g0a, 1), (g0b, 0), (g0b, 1)],
+            [(g00, 0), (g01, 0), (g0b, 0), (g0b, 1)],
             [(g1a, 0), (g1a, 1), (g1a, 2), (g1b, 0)],
         ]
 
@@ -158,9 +157,12 @@ def tile_windowattentionblock_pb_s_kernel(tc, attn_ctx, x, wo, bo, grad_out, out
                 in_=a_grouped[s][:, cols, :].rearrange("p w j -> p (w j)"),
             )
 
-        acc = [sums.tile([M_TILE, CHANNELS], F32, name="acc%d" % m) for m in range(m_tiles)]
+        acc = {}
 
         def multiply(s, m):
+            if s == 0:
+                bank = turns.tile([M_TILE, CHANNELS], F32, name="bank")
+                acc[m] = bank
             m_cols = slice(m * M_TILE, (m + 1) * M_TILE)
             nc.tensor.matmul_mx(
                 out=acc[m][:],
@@ -186,39 +188,36 @@ def tile_windowattentionblock_pb_s_kernel(tc, attn_ctx, x, wo, bo, grad_out, out
         second_turn(0, 0)
         second_turn(0, 1)
         regroup_attn(0, 0, 2, "V")
+        regroup_attn(0, 3, 4, "S")
         for t in range(GROUPS):
             first_turn(1, t)
         second_copy(0, 0, "S")
-        second_copy(0, 1, "S")
-        regroup_attn(0, 2, 4, "V")
-        first_copy(1, 0, "S")
-        first_copy(1, 1, "S")
-        first_copy(1, 2, "S")
+        regroup_attn(0, 2, 3, "V")
         quantise_attn(0, 0, 4)
-        first_copy(1, 3, "V")
+        for t in range(GROUPS):
+            first_copy(1, t, "S")
+        second_copy(0, 1, "V")
         quantise_grad(0, 0)
         quantise_grad(0, 1)
         second_turn(1, 0)
         second_turn(1, 1)
-        for m in range(m_tiles):
-            multiply(0, m)
         regroup_attn(1, 0, 1, "V")
         regroup_attn(1, 1, 2, "V")
-        quantise_attn(1, 0, 1)
-        quantise_attn(1, 1, 2)
+        for m in range(m_tiles):
+            multiply(0, m)
+        regroup_attn(1, 2, 3, "V")
         second_copy(1, 0, "S")
         second_copy(1, 1, "S")
+        quantise_attn(1, 0, 2)
         quantise_grad(1, 0)
-        regroup_attn(1, 2, 3, "V")
         quantise_grad(1, 1)
+        regroup_attn(1, 3, 4, "S")
         multiply(1, 0)
         multiply(1, 1)
-        quantise_attn(1, 2, 3)
+        quantise_attn(1, 2, 4)
         multiply(1, 2)
-        store(0, "S")
-        regroup_attn(1, 3, 4, "V")
-        store(1, "S")
-        quantise_attn(1, 3, 4)
         multiply(1, 3)
-        store(2, "V")
-        store(3, "S")
+        store(0, "S")
+        store(1, "V")
+        store(2, "S")
+        store(3, "V")

@@ -20,6 +20,7 @@ M_TILE = 128
 RUN = PACK * CHANNELS
 GROUPS = 4
 CHUNKS = CHANNELS // P
+WARM_UP = 6
 
 
 def window_order_permutation(nc, pool, ident):
@@ -72,6 +73,12 @@ def tile_windowattentionblock_pb_s_kernel(tc, attn_ctx, x, wo, bo, grad_out, out
             [(g00, 0), (g01, 0), (g0b, 0), (g0b, 1)],
             [(g1a, 0), (g1a, 1), (g1a, 2), (g1b, 0)],
         ]
+
+        zeros = keep.tile([P, P], F32, name="zeros")
+        nc.vector.memset(zeros[:], 0.0)
+        idle_bank = turns.tile([P, P], F32, name="bank")
+        for i in range(WARM_UP):
+            nc.tensor.matmul(out=idle_bank[:], lhsT=zeros[:], rhs=zeros[:], start=True, stop=True)
 
         ident16 = keep.tile([P, P], BF16, name="ident16")
         make_identity(nc, ident16[:])

@@ -20,7 +20,7 @@ M_TILE = 128
 RUN = PACK * CHANNELS
 GROUPS = 4
 CHUNKS = CHANNELS // P
-WARM_UP = 6
+WARM_UP = 4
 
 
 def window_order_permutation(nc, pool, ident):
@@ -77,8 +77,12 @@ def tile_windowattentionblock_pb_s_kernel(tc, attn_ctx, x, wo, bo, grad_out, out
         zeros = keep.tile([P, P], F32, name="zeros")
         nc.vector.memset(zeros[:], 0.0)
         idle_bank = turns.tile([P, P], F32, name="bank")
-        for i in range(WARM_UP):
+
+        def keep_warm():
             nc.tensor.matmul(out=idle_bank[:], lhsT=zeros[:], rhs=zeros[:], start=True, stop=True)
+
+        for i in range(WARM_UP):
+            keep_warm()
 
         ident16 = keep.tile([P, P], BF16, name="ident16")
         make_identity(nc, ident16[:])
@@ -95,6 +99,8 @@ def tile_windowattentionblock_pb_s_kernel(tc, attn_ctx, x, wo, bo, grad_out, out
             for k in range(CHUNKS):
                 nc.tensor.transpose(out=bank[:, k, :], in_=raw[:, i, k * P : (k + 1) * P], identity=perm[:])
             first_banks[(s, t)] = bank
+            if t % 2 == 1:
+                keep_warm()
 
         def first_copy(s, t, engine):
             bank = first_banks[(s, t)]
@@ -115,6 +121,7 @@ def tile_windowattentionblock_pb_s_kernel(tc, attn_ctx, x, wo, bo, grad_out, out
                         out=bank[:, k, u, :], in_=by_channel[s][:, 2 * (2 * b + k) + u, :], identity=ident32[:]
                     )
             second_banks[(s, b)] = bank
+            keep_warm()
 
         g_grouped = [
             [keep.tile([P, 2 * P, PACK], BF16, name="g_grouped%d%d" % (s, b), align_bytes=64) for b in range(2)]

@@ -99,8 +99,6 @@ def tile_windowattentionblock_pb_s_kernel(tc, attn_ctx, x, wo, bo, grad_out, out
             for k in range(CHUNKS):
                 nc.tensor.transpose(out=bank[:, k, :], in_=raw[:, i, k * P : (k + 1) * P], identity=perm[:])
             first_banks[(s, t)] = bank
-            if t % 2 == 1:
-                keep_warm()
 
         def first_copy(s, t, engine):
             bank = first_banks[(s, t)]
@@ -121,7 +119,6 @@ def tile_windowattentionblock_pb_s_kernel(tc, attn_ctx, x, wo, bo, grad_out, out
                         out=bank[:, k, u, :], in_=by_channel[s][:, 2 * (2 * b + k) + u, :], identity=ident32[:]
                     )
             second_banks[(s, b)] = bank
-            keep_warm()
 
         g_grouped = [
             [keep.tile([P, 2 * P, PACK], BF16, name="g_grouped%d%d" % (s, b), align_bytes=64) for b in range(2)]
@@ -195,35 +192,41 @@ def tile_windowattentionblock_pb_s_kernel(tc, attn_ctx, x, wo, bo, grad_out, out
 
         for t in range(GROUPS):
             first_turn(0, t)
+        keep_warm()
+        keep_warm()
         first_copy(0, 0, "S")
         first_copy(0, 1, "V")
         first_copy(0, 2, "S")
         first_copy(0, 3, "V")
         second_turn(0, 0)
         second_turn(0, 1)
+        keep_warm()
+        keep_warm()
         regroup_attn(0, 0, 2, "V")
         regroup_attn(0, 3, 4, "S")
         for t in range(GROUPS):
             first_turn(1, t)
+        keep_warm()
+        keep_warm()
         second_copy(0, 0, "S")
         regroup_attn(0, 2, 3, "V")
         quantise_attn(0, 0, 4)
         for t in range(GROUPS):
             first_copy(1, t, "S")
-        second_copy(0, 1, "V")
         quantise_grad(0, 0)
-        quantise_grad(0, 1)
+        second_copy(0, 1, "S")
         second_turn(1, 0)
         second_turn(1, 1)
         regroup_attn(1, 0, 1, "V")
         regroup_attn(1, 1, 2, "V")
+        quantise_grad(0, 1)
         for m in range(m_tiles):
             multiply(0, m)
-        regroup_attn(1, 2, 3, "V")
         second_copy(1, 0, "S")
         second_copy(1, 1, "S")
         quantise_attn(1, 0, 2)
         quantise_grad(1, 0)
+        regroup_attn(1, 2, 3, "V")
         quantise_grad(1, 1)
         regroup_attn(1, 3, 4, "S")
         multiply(1, 0)

@@ -20,7 +20,6 @@ M_TILE = 128
 RUN = PACK * CHANNELS
 GROUPS = 4
 CHUNKS = CHANNELS // P
-WARM_UP = 4
 
 
 def window_order_permutation(nc, pool, ident):
@@ -43,7 +42,7 @@ def tile_windowattentionblock_pb_s_kernel(tc, attn_ctx, x, wo, bo, grad_out, out
     out_rows = out.rearrange("h d c -> (h d) c")
     m_tiles = FEATURES // M_TILE
 
-    with tc.tile_pool(name="keep", bufs=1) as keep, tc.psum_pool(name="turns", bufs=8) as turns, tc.manual_schedule():
+    with tc.tile_pool(name="keep", bufs=1) as keep, tc.psum_pool(name="turns", bufs=7) as turns, tc.manual_schedule():
 
         def copy_on(engine, out_ap, in_ap):
             if engine == "V":
@@ -76,13 +75,10 @@ def tile_windowattentionblock_pb_s_kernel(tc, attn_ctx, x, wo, bo, grad_out, out
 
         zeros = keep.tile([P, P], F32, name="zeros")
         nc.vector.memset(zeros[:], 0.0)
-        idle_bank = turns.tile([P, P], F32, name="bank")
+        idle_bank = turns.tile([P, P], F32, name="idle_bank", bufs=1)
 
         def keep_warm():
             nc.tensor.matmul(out=idle_bank[:], lhsT=zeros[:], rhs=zeros[:], start=True, stop=True)
-
-        for i in range(WARM_UP):
-            keep_warm()
 
         ident16 = keep.tile([P, P], BF16, name="ident16")
         make_identity(nc, ident16[:])
@@ -190,43 +186,50 @@ def tile_windowattentionblock_pb_s_kernel(tc, attn_ctx, x, wo, bo, grad_out, out
             copy_on(engine, result[:], acc[m][:])
             nc.sync.dma_start(out=out_rows[m * M_TILE : (m + 1) * M_TILE, :], in_=result[:])
 
-        for t in range(GROUPS):
-            first_turn(0, t)
-        keep_warm()
-        keep_warm()
+        for i in range(3):
+            keep_warm()
+        first_turn(0, 0)
+        first_turn(0, 1)
+        first_turn(0, 2)
+        first_turn(0, 3)
+        for i in range(2):
+            keep_warm()
         first_copy(0, 0, "S")
         first_copy(0, 1, "V")
         first_copy(0, 2, "S")
         first_copy(0, 3, "V")
         second_turn(0, 0)
         second_turn(0, 1)
-        keep_warm()
-        keep_warm()
         regroup_attn(0, 0, 2, "V")
         regroup_attn(0, 3, 4, "S")
-        for t in range(GROUPS):
-            first_turn(1, t)
-        keep_warm()
-        keep_warm()
         second_copy(0, 0, "S")
         regroup_attn(0, 2, 3, "V")
-        quantise_attn(0, 0, 4)
-        for t in range(GROUPS):
-            first_copy(1, t, "S")
-        quantise_grad(0, 0)
         second_copy(0, 1, "S")
+        first_turn(1, 0)
+        first_turn(1, 1)
+        first_turn(1, 2)
+        first_turn(1, 3)
+        for i in range(2):
+            keep_warm()
+        quantise_attn(0, 0, 4)
+        first_copy(1, 0, "V")
+        first_copy(1, 1, "S")
+        first_copy(1, 2, "V")
+        first_copy(1, 3, "S")
         second_turn(1, 0)
         second_turn(1, 1)
-        regroup_attn(1, 0, 1, "V")
-        regroup_attn(1, 1, 2, "V")
+        quantise_grad(0, 0)
         quantise_grad(0, 1)
-        for m in range(m_tiles):
-            multiply(0, m)
+        regroup_attn(1, 0, 2, "V")
+        multiply(0, 0)
+        multiply(0, 1)
+        multiply(0, 2)
+        multiply(0, 3)
         second_copy(1, 0, "S")
         second_copy(1, 1, "S")
-        quantise_attn(1, 0, 2)
-        quantise_grad(1, 0)
         regroup_attn(1, 2, 3, "V")
+        quantise_grad(1, 0)
+        quantise_attn(1, 0, 2)
         quantise_grad(1, 1)
         regroup_attn(1, 3, 4, "S")
         multiply(1, 0)

@@ -63,9 +63,9 @@ def tile_windowattentionblock_pb_s_kernel(tc, attn_ctx, x, wo, bo, grad_out, out
         g00 = load_grad("g00", 1, 1)
         g01 = load_grad("g01", 2, 1)
         g0b = load_grad("g0b", 3, 2)
-        a_raw0 = load_attn(0)
         g1a = load_grad("g1a", 5, 3)
         g1b = load_grad("g1b", 0, 1)
+        a_raw0 = load_attn(0)
         a_raw1 = load_attn(1)
         attn_raw = [a_raw0, a_raw1]
         grad_group = [
@@ -198,46 +198,55 @@ def tile_windowattentionblock_pb_s_kernel(tc, attn_ctx, x, wo, bo, grad_out, out
         first_copy(0, 1, "V")
         first_copy(0, 2, "S")
         first_copy(0, 3, "V")
-        second_turn(0, 0)
-        second_turn(0, 1)
-        regroup_attn(0, 0, 2, "V")
-        regroup_attn(0, 3, 4, "S")
-        second_copy(0, 0, "S")
-        regroup_attn(0, 2, 3, "V")
-        second_copy(0, 1, "S")
         first_turn(1, 0)
         first_turn(1, 1)
         first_turn(1, 2)
         first_turn(1, 3)
-        for i in range(2):
-            keep_warm()
-        quantise_attn(0, 0, 4)
-        first_copy(1, 0, "V")
-        first_copy(1, 1, "S")
-        first_copy(1, 2, "V")
-        first_copy(1, 3, "S")
+        second_turn(0, 0)
+        second_turn(0, 1)
+        first_copy(1, 0, "S")
+        first_copy(1, 1, "V")
+        first_copy(1, 2, "S")
+        first_copy(1, 3, "V")
         second_turn(1, 0)
         second_turn(1, 1)
+        for i in range(3):
+            keep_warm()
+        second_copy(0, 0, "S")
+        regroup_attn(0, 0, 1, "V")
+        second_copy(0, 1, "S")
         quantise_grad(0, 0)
-        quantise_grad(0, 1)
-        regroup_attn(1, 0, 2, "V")
-        multiply(0, 0)
-        multiply(0, 1)
-        multiply(0, 2)
-        multiply(0, 3)
         second_copy(1, 0, "S")
+        quantise_attn(0, 0, 1)
+        quantise_grad(0, 1)
         second_copy(1, 1, "S")
-        regroup_attn(1, 2, 3, "V")
+        multiply(0, 0)
+        for i in range(2):
+            keep_warm()
+        regroup_attn(1, 0, 1, "V")
+        regroup_attn(0, 1, 2, "S")
         quantise_grad(1, 0)
-        quantise_attn(1, 0, 2)
         quantise_grad(1, 1)
-        regroup_attn(1, 3, 4, "S")
+        quantise_attn(1, 0, 1)
         multiply(1, 0)
+        regroup_attn(1, 1, 2, "V")
+        regroup_attn(0, 2, 3, "S")
+        quantise_attn(0, 1, 2)
+        quantise_attn(1, 1, 2)
+        multiply(0, 1)
         multiply(1, 1)
-        quantise_attn(1, 2, 4)
-        multiply(1, 2)
-        multiply(1, 3)
         store(0, "S")
-        store(1, "V")
+        regroup_attn(1, 2, 3, "V")
+        quantise_attn(0, 2, 3)
+        quantise_attn(1, 2, 3)
+        multiply(0, 2)
+        multiply(1, 2)
+        regroup_attn(0, 3, 4, "V")
+        regroup_attn(1, 3, 4, "V")
+        store(1, "S")
+        quantise_attn(0, 3, 4)
+        quantise_attn(1, 3, 4)
+        multiply(0, 3)
+        multiply(1, 3)
         store(2, "S")
         store(3, "V")

@@ -152,8 +152,8 @@ def tile_windowattentionblock_pb_s_kernel(tc, attn_ctx, x, wo, bo, grad_out, out
             a_tokens = attn_raw[s][:].rearrange("p (j w) -> p j w", j=PACK)
             copy_on(
                 engine,
-                a_grouped[s][:, cols, :].rearrange("p (c i) j -> p c j i", i=4),
-                a_tokens[:, :, cols].rearrange("p j (c i) -> p c j i", i=4),
+                a_grouped[s][:, cols, :],
+                a_tokens[:, :, cols].rearrange("p j c -> p c j"),
             )
 
         def quantise_attn(s, m0, m1):
@@ -181,10 +181,13 @@ def tile_windowattentionblock_pb_s_kernel(tc, attn_ctx, x, wo, bo, grad_out, out
                 stop=(s == PASSES - 1),
             )
 
-        def store(m, engine):
-            result = keep.tile([M_TILE, CHANNELS], F32, name="result%d" % m)
-            copy_on(engine, result[:], acc[m][:])
-            nc.sync.dma_start(out=out_rows[m * M_TILE : (m + 1) * M_TILE, :], in_=result[:])
+        def store(m, engine, parts=1):
+            width = CHANNELS // parts
+            for i in range(parts):
+                cols = slice(i * width, (i + 1) * width)
+                result = keep.tile([M_TILE, width], F32, name="result%d_%d" % (m, i))
+                copy_on(engine, result[:], acc[m][:, cols])
+                nc.sync.dma_start(out=out_rows[m * M_TILE : (m + 1) * M_TILE, cols], in_=result[:])
 
         for i in range(3):
             keep_warm()
@@ -249,4 +252,4 @@ def tile_windowattentionblock_pb_s_kernel(tc, attn_ctx, x, wo, bo, grad_out, out
         multiply(0, 3)
         multiply(1, 3)
         store(2, "S")
-        store(3, "V")
+        store(3, "V", parts=2)

from concourse import mybir
from concourse.masks import make_identity

FLOPS = 2 * 1024 * 512 * 512
BYTES = (1024 * 512 * 2) * 2 + 512 * 512 * 4

BF16 = mybir.dt.bfloat16
F32 = mybir.dt.float32
U32 = mybir.dt.uint32
U8 = mybir.dt.uint8
E4M3X4 = mybir.dt.float8_e4m3fn_x4
E5M2X4 = mybir.dt.float8_e5m2_x4

P = 128
PACK = 4
PASSES = 2
FEATURES = 512
CHANNELS = 512
M_TILE = 128
RUN = PACK * CHANNELS
GROUPS = 4
CHUNKS = CHANNELS // P


def window_order_permutation(nc, pool, ident):
    perm = pool.tile([P, P], BF16, name="perm")
    to_token = perm[:].rearrange("q (u g r h v) -> q u h g r v", u=2, g=4, r=4, h=2, v=2)
    from_pixel = ident[:].rearrange("q (r g e u v) -> q u e g r v", r=4, g=4, e=2, u=2, v=2)
    for u in range(2):
        nc.vector.tensor_copy(out=to_token[:, u, 0], in_=from_pixel[:, u, 1])
        nc.vector.tensor_copy(out=to_token[:, u, 1, 0:3], in_=from_pixel[:, u, 0, 1:4])
        nc.vector.tensor_copy(out=to_token[:, u, 1, 3:4], in_=from_pixel[:, u, 0, 0:1])
    return perm


def tile_windowattentionblock_pb_s_kernel(tc, attn_ctx, x, wo, bo, grad_out, out):
    nc = tc.nc
    attn_runs = attn_ctx.rearrange("n t h d -> (n t) (h d)").rearrange(
        "(s p j) f -> s p (j f)", s=PASSES, p=P, j=PACK
    )
    grad_px = grad_out.rearrange("b (t r) j c -> (b r j) t c", r=4)
    out_rows = out.rearrange("h d c -> (h d) c")
    m_tiles = FEATURES // M_TILE

    with tc.tile_pool(name="keep", bufs=1) as keep, tc.psum_pool(name="turns", bufs=7) as turns, tc.manual_schedule():

        def copy_on(engine, out_ap, in_ap):
            if engine == "V":
                nc.vector.tensor_copy(out=out_ap, in_=in_ap)
            else:
                nc.scalar.copy(out=out_ap, in_=in_ap)

        def load_grad(name, first_group, groups):
            raw = keep.tile([P, groups, CHANNELS], BF16, name=name)
            nc.sync.dma_start(out=raw[:], in_=grad_px[:, first_group : first_group + groups, :])
            return raw

        def load_attn(s):
            a_raw = keep.tile([P, RUN], BF16, name="a_raw%d" % s)
            nc.sync.dma_start(out=a_raw[:], in_=attn_runs[s])
            return a_raw

        g00 = load_grad("g00", 1, 1)
        g01 = load_grad("g01", 2, 1)
        g0b = load_grad("g0b", 3, 2)
        g1a = load_grad("g1a", 5, 3)
        g1b = load_grad("g1b", 0, 1)
        a_raw0 = load_attn(0)
        a_raw1 = load_attn(1)
        attn_raw = [a_raw0, a_raw1]
        grad_group = [
            [(g00, 0), (g01, 0), (g0b, 0), (g0b, 1)],
            [(g1a, 0), (g1a, 1), (g1a, 2), (g1b, 0)],
        ]

        zeros = keep.tile([P, P], F32, name="zeros")
        nc.vector.memset(zeros[:], 0.0)
        idle_bank = turns.tile([P, P], F32, name="idle_bank", bufs=1)

        def keep_warm():
            nc.tensor.matmul(out=idle_bank[:], lhsT=zeros[:], rhs=zeros[:], start=True, stop=True)

        ident16 = keep.tile([P, P], BF16, name="ident16")
        make_identity(nc, ident16[:])
        perm = window_order_permutation(nc, keep, ident16)
        ident32 = keep.tile([P, P], F32, name="ident32")
        make_identity(nc, ident32[:])

        by_channel = [keep.tile([P, 2 * CHUNKS, P], F32, name="by_channel%d" % s) for s in range(PASSES)]
        first_banks = {}

        def first_turn(s, t):
            raw, i = grad_group[s][t]
            bank = turns.tile([P, CHUNKS, P], BF16, name="bank")
            for k in range(CHUNKS):
                nc.tensor.transpose(out=bank[:, k, :], in_=raw[:, i, k * P : (k + 1) * P], identity=perm[:])
            first_banks[(s, t)] = bank

        def first_copy(s, t, engine):
            bank = first_banks[(s, t)]
            words = bank[:].rearrange("c k n -> c (k n)").bitcast(F32)
            half, u = divmod(t, 2)
            dest = by_channel[s][:, :, half * 64 : (half + 1) * 64].rearrange(
                "c y (g u w) -> c y g u w", g=4, u=2, w=8
            )
            copy_on(engine, dest[:, :, :, u, :], words.rearrange("c (y g w) -> c y g w", g=4, w=8))

        second_banks = {}

        def second_turn(s, b):
            bank = turns.tile([P, 2, 2, P], F32, name="bank")
            for k in range(2):
                for u in range(2):
                    nc.tensor.transpose(
                        out=bank[:, k, u, :], in_=by_channel[s][:, 2 * (2 * b + k) + u, :], identity=ident32[:]
                    )
            second_banks[(s, b)] = bank

        g_grouped = [
            [keep.tile([P, 2 * P, PACK], BF16, name="g_grouped%d%d" % (s, b), align_bytes=64) for b in range(2)]
            for s in range(PASSES)
        ]

        def second_copy(s, b, engine):
            bank = second_banks[(s, b)]
            dest = g_grouped[s][b][:].rearrange("p c j -> p (c j)").bitcast(F32)
            copy_on(
                engine,
                dest.rearrange("p (k c u) -> p k c u", k=2, u=2),
                bank[:].rearrange("p k u c -> p k c u"),
            )

        g_codes = [keep.tile([P, CHANNELS], U32, name="g_codes%d" % s, align_bytes=64) for s in range(PASSES)]
        g_scales = [keep.tile([P, CHANNELS], U8, name="g_scales%d" % s, align_bytes=64) for s in range(PASSES)]
        a_codes = [keep.tile([P, FEATURES], U32, name="a_codes%d" % s, align_bytes=64) for s in range(PASSES)]
        a_scales = [keep.tile([P, FEATURES], U8, name="a_scales%d" % s, align_bytes=64) for s in range(PASSES)]

        def quantise_grad(s, b):
            cols = slice(b * 2 * P, (b + 1) * 2 * P)
            nc.vector.quantize_mx(
                out=g_codes[s][:, cols].bitcast(E5M2X4),
                scales=g_scales[s][:, cols],
                in_=g_grouped[s][b][:].rearrange("p c j -> p (c j)"),
            )

        a_grouped = [
            keep.tile([P, FEATURES, PACK], BF16, name="a_grouped%d" % s, align_bytes=64) for s in range(PASSES)
        ]

        def regroup_attn(s, m0, m1, engine):
            cols = slice(m0 * M_TILE, m1 * M_TILE)
            a_tokens = attn_raw[s][:].rearrange("p (j w) -> p j w", j=PACK)
            copy_on(
                engine,
                a_grouped[s][:, cols, :],
                a_tokens[:, :, cols].rearrange("p j c -> p c j"),
            )

        def quantise_attn(s, m0, m1):
            cols = slice(m0 * M_TILE, m1 * M_TILE)
            nc.vector.quantize_mx(
                out=a_codes[s][:, cols].bitcast(E4M3X4),
                scales=a_scales[s][:, cols],
                in_=a_grouped[s][:, cols, :].rearrange("p w j -> p (w j)"),
            )

        acc = {}

        def multiply(s, m):
            if s == 0:
                bank = turns.tile([M_TILE, CHANNELS], F32, name="bank")
                acc[m] = bank
            m_cols = slice(m * M_TILE, (m + 1) * M_TILE)
            nc.tensor.matmul_mx(
                out=acc[m][:],
                lhsT=a_codes[s][:, m_cols].bitcast(E4M3X4),
                lhsT_scale=a_scales[s][:, m_cols],
                rhs=g_codes[s][:].bitcast(E5M2X4),
                rhs_scale=g_scales[s][:],
                start=(s == 0),
                stop=(s == PASSES - 1),
            )

        def store(m, engine, parts=1):
            width = CHANNELS // parts
            for i in range(parts):
                cols = slice(i * width, (i + 1) * width)
                result = keep.tile([M_TILE, width], F32, name="result%d_%d" % (m, i))
                copy_on(engine, result[:], acc[m][:, cols])
                nc.sync.dma_start(out=out_rows[m * M_TILE : (m + 1) * M_TILE, cols], in_=result[:])

        for i in range(3):
            keep_warm()
        first_turn(0, 0)
        first_turn(0, 1)
        first_turn(0, 2)
        first_turn(0, 3)
        for i in range(2):
            keep_warm()
        first_copy(0, 0, "S")
        first_copy(0, 1, "V")
        first_copy(0, 2, "S")
        first_copy(0, 3, "V")
        first_turn(1, 0)
        first_turn(1, 1)
        first_turn(1, 2)
        first_turn(1, 3)
        second_turn(0, 0)
        second_turn(0, 1)
        first_copy(1, 0, "S")
        first_copy(1, 1, "V")
        first_copy(1, 2, "S")
        first_copy(1, 3, "V")
        second_turn(1, 0)
        second_turn(1, 1)
        for i in range(3):
            keep_warm()
        second_copy(0, 0, "S")
        regroup_attn(0, 0, 1, "V")
        second_copy(0, 1, "S")
        quantise_grad(0, 0)
        second_copy(1, 0, "S")
        quantise_attn(0, 0, 1)
        quantise_grad(0, 1)
        second_copy(1, 1, "S")
        multiply(0, 0)
        for i in range(2):
            keep_warm()
        regroup_attn(1, 0, 1, "V")
        regroup_attn(0, 1, 2, "S")
        quantise_grad(1, 0)
        quantise_grad(1, 1)
        quantise_attn(1, 0, 1)
        multiply(1, 0)
        regroup_attn(1, 1, 2, "V")
        regroup_attn(0, 2, 3, "S")
        quantise_attn(0, 1, 2)
        quantise_attn(1, 1, 2)
        multiply(0, 1)
        multiply(1, 1)
        store(0, "S")
        regroup_attn(1, 2, 3, "V")
        quantise_attn(0, 2, 3)
        quantise_attn(1, 2, 3)
        multiply(0, 2)
        multiply(1, 2)
        regroup_attn(0, 3, 4, "V")
        regroup_attn(1, 3, 4, "V")
        store(1, "S")
        quantise_attn(0, 3, 4)
        quantise_attn(1, 3, 4)
        multiply(0, 3)
        multiply(1, 3)
        store(2, "S")
        store(3, "V", parts=2)
